import numpy as np
import ml_dtypes


def mxq(x, axis, fmt="e4m3"):
    dtype, down = {"e4m3": (ml_dtypes.float8_e4m3fn, 7), "e5m2": (ml_dtypes.float8_e5m2, 14)}[fmt]
    v = np.moveaxis(np.asarray(x, np.float32).astype(ml_dtypes.bfloat16).astype(np.float64), axis, -1)
    blocks = v.reshape(v.shape[:-1] + (-1, 32))
    amax = np.abs(blocks).max(-1, keepdims=True)
    byte = np.maximum(np.where(amax > 0, np.frexp(amax)[1] - 1 + 127, 0) - down, 1)
    scale = np.exp2(byte - 127.0)
    codes = (blocks / scale).astype(np.float32).astype(dtype).astype(np.float64)
    return np.moveaxis((codes * scale).reshape(v.shape), -1, axis)


WIDE = False


def mx_kscale(k):
    if not WIDE:
        return np.ones(k)
    levels = np.array([10, -10, 5, -5, 0])
    if k % 512:
        return np.exp2(np.random.permutation(np.resize(levels, k // 32))).repeat(32)
    a = np.empty((k // 512, 16))
    for p in range(k // 512):
        a[p, :8] = np.random.permutation(np.resize(levels, 8))
        for g in range(8):
            far = levels[np.abs(levels - a[p, g]) >= 10]
            a[p, g + 8] = far[np.random.randint(len(far))]
    return np.exp2(a.ravel()).repeat(32)


BF16 = ml_dtypes.bfloat16


def bf(x):
    return np.asarray(x, np.float32).astype(BF16)


def f64(x):
    return np.asarray(x).astype(np.float64)


B, C_IN, N, L, C_OUT, ORDER, EMBED, SUP_LEN = 4, 32, 1024, 12, 64, 3, 10, 2


def setup_inputs():
    s = mx_kscale(N)
    return {"a": bf(np.random.standard_normal((N, N)) / np.sqrt(N) * s[None, :] / s[:, None]),
            "x": bf(np.random.standard_normal((B, C_IN, N, L)) / s[None, None, :, None])}


def reference(a, x):
    a, x = f64(a), f64(x)
    a_left = mxq(a, 1, "e4m3")
    xq = mxq(x, 2, "e4m3")
    t2 = 2.0 * (a_left @ mxq(a, 0, "e4m3")) - np.eye(N)
    y1 = a_left @ xq
    y2 = mxq(t2, 1, "e4m3") @ xq
    return np.stack([y1, y2], axis=1).transpose(0, 1, 3, 2, 4)

@@ -1,0 +1,227 @@
+from contextlib import ExitStack
+
+import concourse.mybir as mybir
+from concourse.masks import make_identity
+
+F32 = mybir.dt.float32
+BF16 = mybir.dt.bfloat16
+U32 = mybir.dt.uint32
+U8 = mybir.dt.uint8
+FP8X4 = mybir.dt.float8_e4m3fn_x4
+ALU = mybir.AluOpType
+ACT = mybir.ActivationFunctionType
+
+P = 128
+TILES = 8
+PASSES = 2
+SLOTS = 4
+NODES = 1024
+STEP_PAIRS = 6
+COLS = 1536
+CHUNK = 512
+CHUNKS = COLS // CHUNK
+ROW_WORDS = NODES // 2
+FLOPS = 2 * NODES * NODES * (NODES + 2 * COLS)
+
+
+def tile_gcn_pa_kernel(tc, a, x, out):
+    nc = tc.nc
+    with ExitStack() as ctx:
+        ctx.enter_context(tc.manual_schedule())
+        keep = ctx.enter_context(tc.tile_pool(name="keep", bufs=1))
+        results = ctx.enter_context(tc.tile_pool(name="results", bufs=8))
+        psum = ctx.enter_context(tc.psum_pool(name="psum", bufs=8))
+
+        def new_bank():
+            bank = psum.tile([P, CHUNK], F32, name="bank", tag="bank")
+            return bank
+
+        def copy(engine, dst, src):
+            if engine == "vector":
+                nc.vector.tensor_copy(out=dst, in_=src)
+            else:
+                nc.scalar.copy(out=dst, in_=src)
+
+        def quantise(codes, scales, grouped, first, width):
+            nc.vector.quantize_mx(
+                out=codes[:, first : first + width].bitcast(FP8X4),
+                scales=scales[:, first : first + width],
+                in_=grouped[:, SLOTS * first : SLOTS * (first + width)],
+            )
+
+        def mx_pass(acc, left, left_first, right, right_first, width, g):
+            nc.tensor.matmul_mx(
+                out=acc,
+                lhsT=left[0][:, left_first : left_first + P].bitcast(FP8X4),
+                lhsT_scale=left[1][:, left_first : left_first + P],
+                rhs=right[0][:, right_first : right_first + width].bitcast(FP8X4),
+                rhs_scale=right[1][:, right_first : right_first + width],
+                start=(g == 0),
+                stop=(g == PASSES - 1),
+            )
+
+        eye_strip = keep.tile([P, 7 * P], F32, name="eye_strip")
+        nc.gpsimd.memset(eye_strip[:], 0.0)
+        make_identity(nc, eye_strip[:, 3 * P : 4 * P], nomemset=True)
+        identity = eye_strip[:, 3 * P : 4 * P]
+
+        x_rows = keep.tile([P, NODES * 12], BF16, name="x_rows")
+        a_rows = keep.tile([P, TILES * NODES], BF16, name="a_rows")
+        x_flat = x.rearrange("b c m l -> (b c) (m l)")
+        for q in range(4):
+            piece = slice(3072 * q, 3072 * (q + 1))
+            nc.sync.dma_start(out=x_rows[:, piece], in_=x_flat[:, piece])
+        for q in range(4):
+            g, u = q // 2, q % 2
+            nc.sync.dma_start(
+                out=a_rows[:, 2048 * q : 2048 * (q + 1)].rearrange("p (e m) -> p e m", e=2),
+                in_=a[512 * g : 512 * (g + 1), :].rearrange("(p t) m -> p t m", t=SLOTS)[:, 2 * u : 2 * u + 2, :],
+            )
+
+        def operand(name, columns):
+            grouped = keep.tile([P, SLOTS * columns], BF16, name=name + "_grouped", align_bytes=64)
+            codes = keep.tile([P, columns], U32, name=name + "_codes", align_bytes=64)
+            scales = keep.tile([P, columns], U8, name=name + "_scales", align_bytes=64)
+            return grouped, (codes, scales)
+
+        x_grouped, x_mx = operand("x", PASSES * COLS)
+        left_grouped, left_mx = operand("left", PASSES * NODES)
+        right_grouped, right_mx = operand("right", PASSES * NODES)
+        t2_grouped, t2_mx = operand("t2", PASSES * NODES)
+
+        x_words = x_rows[:].bitcast(F32).rearrange("b (g p t h) -> b g t h p", g=PASSES, p=P, t=SLOTS, h=STEP_PAIRS)
+        x_banks = {}
+
+        def x_transposes(g, u):
+            for h in range(STEP_PAIRS):
+                if u == 0:
+                    x_banks[(g, h)] = new_bank()
+                for e in range(2):
+                    t = 2 * u + e
+                    nc.tensor.transpose(x_banks[(g, h)][:, t * P : (t + 1) * P], x_words[:, g, t, h, :], identity)
+
+        def x_regroup(g, h, engine):
+            first = SLOTS * (g * COLS + h * 2 * P)
+            copy(
+                engine,
+                x_grouped[:, first : first + SLOTS * 2 * P].rearrange("p (b k t) -> p b k t", k=2, t=SLOTS),
+                x_banks[(g, h)][:].bitcast(BF16).rearrange("p (t b k) -> p b k t", t=SLOTS, k=2),
+            )
+
+        def x_quantise(g, c):
+            quantise(x_mx[0], x_mx[1], x_grouped, g * COLS + c * CHUNK, CHUNK)
+
+        a_words = a_rows[:].bitcast(F32)
+        left_words = left_grouped[:].bitcast(F32)
+
+        def left_tile(tau):
+            bank = new_bank()
+            for i in range(4):
+                first = tau * ROW_WORDS + i // 2 * 2 * P
+                nc.tensor.transpose(bank[:, i * P : (i + 1) * P], a_words[:, first + i % 2 : first + 2 * P : 2], identity)
+            copy(
+                "scalar",
+                left_words[:, tau * ROW_WORDS : (tau + 1) * ROW_WORDS].rearrange("p (g n u) -> p g n u", g=PASSES, u=2),
+                bank[:].rearrange("p (g u n) -> p g n u", g=PASSES, u=2),
+            )
+
+        def left_quantise(tau):
+            quantise(left_mx[0], left_mx[1], left_grouped, tau * PASSES * P, PASSES * P)
+
+        a_by_tile = a_rows[:].rearrange("p (g t h n e) -> p g h e n t", g=PASSES, t=SLOTS, h=PASSES, n=P, e=SLOTS)
+
+        def right_regroup(g, q):
+            first = SLOTS * (g * NODES + q * 2 * P)
+            nc.vector.tensor_copy(
+                out=right_grouped[:, first : first + SLOTS * 2 * P].rearrange("p (e n t) -> p e n t", e=2, t=SLOTS),
+                in_=a_by_tile[:, g, q // 2, 2 * (q % 2) : 2 * (q % 2) + 2],
+            )
+
+        result_tiles = {}
+
+        def y_chunk(term, tau, c, left, engine):
+            bank = new_bank()
+            for g in range(PASSES):
+                mx_pass(bank[:], left, (tau * PASSES + g) * P, x_mx, g * COLS + c * CHUNK, CHUNK, g)
+            if c == 0:
+                result_tiles[(term, tau)] = results.tile([P, COLS], F32, name="result", tag="result")
+            result = result_tiles[(term, tau)]
+            copy(
+                engine,
+                result[:].rearrange("p (b l) -> p b l", l=12)[:, :, 4 * c : 4 * c + 4].rearrange("p b (h k) -> p b h k", k=2),
+                bank[:].rearrange("p (h b k) -> p b h k", h=2, k=2),
+            )
+            if c == CHUNKS - 1:
+                rows = out[:, term].rearrange("b (g p t) c l -> g t p b (c l)", g=PASSES, p=P, t=SLOTS)[tau // SLOTS, tau % SLOTS]
+                nc.sync.dma_start(out=rows, in_=result[:].rearrange("p (b f) -> p b f", b=4))
+
+        def t2_tile(j):
+            for g2 in range(PASSES):
+                bank = new_bank()
+                for t in range(SLOTS):
+                    for g in range(PASSES):
+                        mx_pass(bank[:, t * P : (t + 1) * P], right_mx, g * NODES + (SLOTS * g2 + t) * P,
+                                left_mx, (j * PASSES + g) * P, P, g)
+                first = SLOTS * (j * PASSES + g2) * P
+                dst = t2_grouped[:, first : first + SLOTS * P].rearrange("p (n t) -> p n t", t=SLOTS)
+                src = bank[:].rearrange("p (t n) -> p n t", t=SLOTS)
+                if j // SLOTS == g2:
+                    window = (3 - j % SLOTS) * P
+                    nc.vector.scalar_tensor_tensor(
+                        out=dst, in0=src, scalar=2.0,
+                        in1=eye_strip[:, window : window + SLOTS * P].rearrange("p (t n) -> p n t", t=SLOTS),
+                        op0=ALU.mult, op1=ALU.subtract,
+                    )
+                else:
+                    nc.scalar.activation(out=dst, in_=src, func=ACT.Copy, scale=2.0)
+            quantise(t2_mx[0], t2_mx[1], t2_grouped, j * PASSES * P, PASSES * P)
+
+        x_transposes(0, 0)
+        x_transposes(0, 1)
+        for h in range(STEP_PAIRS):
+            x_regroup(0, h, "vector" if h % 2 == 0 else "scalar")
+            if h == 3:
+                x_quantise(0, 0)
+        x_transposes(1, 0)
+        x_transposes(1, 1)
+        x_regroup(1, 0, "scalar")
+        x_regroup(1, 1, "vector")
+        for tau in range(4):
+            left_tile(tau)
+        x_quantise(1, 0)
+        left_quantise(0)
+        left_quantise(1)
+        x_regroup(1, 2, "scalar")
+        x_regroup(1, 3, "vector")
+        left_quantise(2)
+        left_quantise(3)
+        x_quantise(0, 1)
+        x_quantise(1, 1)
+        x_regroup(1, 4, "scalar")
+        x_regroup(1, 5, "vector")
+        x_quantise(0, 2)
+        x_quantise(1, 2)
+        for tau in range(4):
+            y_chunk(0, tau, 0, left_mx, "scalar")
+        for q in range(4):
+            right_regroup(0, q)
+        for tau in range(4, TILES):
+            left_tile(tau)
+        for tau in range(4, TILES):
+            left_quantise(tau)
+        for c in range(1, CHUNKS):
+            for tau in range(4):
+                y_chunk(0, tau, c, left_mx, "scalar")
+        for q in range(4):
+            right_regroup(1, q)
+        for g in range(PASSES):
+            quantise(right_mx[0], right_mx[1], right_grouped, g * NODES, NODES)
+        for tau in range(4, TILES):
+            for c in range(CHUNKS):
+                y_chunk(0, tau, c, left_mx, "scalar" if tau < TILES - 1 else "vector")
+        for j in range(TILES + 1):
+            if j < TILES:
+                t2_tile(j)
+            if j > 0:
+                for c in range(CHUNKS):
+                    y_chunk(1, j - 1, c, t2_mx, "vector" if (j - 1) % 3 == 1 else "scalar")

@@ -128,14 +128,12 @@ def tile_gcn_pa_kernel(tc, a, x, out):
         def left_quantise(tau):
             quantise(left_mx[0], left_mx[1], left_grouped, tau * PASSES * P, PASSES * P)
 
-        a_by_tile = a_rows[:].rearrange("p (g t h n e) -> p g h e n t", g=PASSES, t=SLOTS, h=PASSES, n=P, e=SLOTS)
+        half_tile = P // 2
+        a_by_tile = a_rows[:].rearrange("p (g t q n e) -> p g q n e t", g=PASSES, t=SLOTS, q=4, n=half_tile, e=SLOTS)
+        right_by_tile = right_grouped[:].rearrange("p (g h e m n t) -> p g h m n e t", g=PASSES, h=PASSES, e=SLOTS, m=2, n=half_tile, t=SLOTS)
 
         def right_regroup(g, q):
-            first = SLOTS * (g * NODES + q * 2 * P)
-            nc.vector.tensor_copy(
-                out=right_grouped[:, first : first + SLOTS * 2 * P].rearrange("p (e n t) -> p e n t", e=2, t=SLOTS),
-                in_=a_by_tile[:, g, q // 2, 2 * (q % 2) : 2 * (q % 2) + 2],
-            )
+            nc.vector.tensor_copy(out=right_by_tile[:, g, q // 2, q % 2], in_=a_by_tile[:, g, q])
 
         result_tiles = {}
 

@@ -65,7 +65,8 @@ def tile_gcn_pa_kernel(tc, a, x, out):
         make_identity(nc, eye_strip[:, 3 * P : 4 * P], nomemset=True)
         identity = eye_strip[:, 3 * P : 4 * P]
 
-        x_rows = keep.tile([P, NODES * 12], BF16, name="x_rows")
+        x_rows = keep.tile([P, NODES * 12], BF16, name="x_rows", align_bytes=64)
+        x_pairs = keep.tile([P, NODES * 12], BF16, name="x_pairs")
         a_rows = keep.tile([P, TILES * NODES], BF16, name="a_rows")
         x_flat = x.rearrange("b c m l -> (b c) (m l)")
         for q in range(4):
@@ -84,28 +85,41 @@ def tile_gcn_pa_kernel(tc, a, x, out):
             scales = keep.tile([P, columns], U8, name=name + "_scales", align_bytes=64)
             return grouped, (codes, scales)
 
-        x_grouped, x_mx = operand("x", PASSES * COLS)
+        x_mx = (
+            keep.tile([P, PASSES * COLS], U32, name="x_codes", align_bytes=64),
+            keep.tile([P, PASSES * COLS], U8, name="x_scales", align_bytes=64),
+        )
+        x_grouped = x_rows
         left_grouped, left_mx = operand("left", PASSES * NODES)
         right_grouped, right_mx = operand("right", PASSES * NODES)
         t2_grouped, t2_mx = operand("t2", PASSES * NODES)
 
-        x_words = x_rows[:].bitcast(F32).rearrange("b (g p t h) -> b g t h p", g=PASSES, p=P, t=SLOTS, h=STEP_PAIRS)
+        x_by_node = x_rows[:].rearrange("b (g p u e r i) -> b g r u p e i", g=PASSES, p=P, u=2, e=2, r=3, i=4)
+        x_by_place = x_pairs[:].rearrange("b (g r i u p e) -> b g r u p e i", g=PASSES, r=3, i=4, u=2, p=P, e=2)
+        pair_words = x_pairs[:].bitcast(F32)
         x_banks = {}
 
-        def x_transposes(g, u):
+        def x_pair_up(g, half):
+            part = slice(half * P // 2, (half + 1) * P // 2)
+            for r in range(3):
+                nc.vector.tensor_copy(out=x_by_place[:, g, r, :, part], in_=x_by_node[:, g, r, :, part])
+
+        def x_transposes(g):
             for h in range(STEP_PAIRS):
-                if u == 0:
-                    x_banks[(g, h)] = new_bank()
-                for e in range(2):
-                    t = 2 * u + e
-                    nc.tensor.transpose(x_banks[(g, h)][:, t * P : (t + 1) * P], x_words[:, g, t, h, :], identity)
+                bank = new_bank()
+                x_banks[(g, h)] = bank
+                for i in range(4):
+                    first = ((g * STEP_PAIRS + h) * 4 + i) * P
+                    nc.tensor.transpose(bank[:, i * P : (i + 1) * P], pair_words[:, first : first + P], identity)
+
+        x_words = x_grouped[:].bitcast(F32)
 
         def x_regroup(g, h, engine):
-            first = SLOTS * (g * COLS + h * 2 * P)
+            first = 2 * (g * COLS + h * 2 * P)
             copy(
                 engine,
-                x_grouped[:, first : first + SLOTS * 2 * P].rearrange("p (b k t) -> p b k t", k=2, t=SLOTS),
-                x_banks[(g, h)][:].bitcast(BF16).rearrange("p (t b k) -> p b k t", t=SLOTS, k=2),
+                x_words[:, first : first + CHUNK].rearrange("p (b k u) -> p b k u", k=2, u=2),
+                x_banks[(g, h)][:].rearrange("p (k u b) -> p b k u", k=2, u=2),
             )
 
         def x_quantise(g, c):
@@ -174,16 +188,17 @@ def tile_gcn_pa_kernel(tc, a, x, out):
                     nc.scalar.activation(out=dst, in_=src, func=ACT.Copy, scale=2.0)
             quantise(t2_mx[0], t2_mx[1], t2_grouped, j * PASSES * P, PASSES * P)
 
-        x_transposes(0, 0)
-        x_transposes(0, 1)
+        x_pair_up(0, 0)
+        x_pair_up(0, 1)
+        x_transposes(0)
         for h in range(STEP_PAIRS):
-            x_regroup(0, h, "vector" if h % 2 == 0 else "scalar")
-            if h == 3:
-                x_quantise(0, 0)
-        x_transposes(1, 0)
-        x_transposes(1, 1)
+            x_regroup(0, h, "scalar")
+        x_pair_up(1, 0)
+        x_pair_up(1, 1)
+        x_quantise(0, 0)
+        x_transposes(1)
         x_regroup(1, 0, "scalar")
-        x_regroup(1, 1, "vector")
+        x_regroup(1, 1, "scalar")
         for tau in range(4):
             left_tile(tau)
         x_quantise(1, 0)

@@ -65,6 +65,10 @@ def tile_gcn_pa_kernel(tc, a, x, out):
         make_identity(nc, eye_strip[:, 3 * P : 4 * P], nomemset=True)
         identity = eye_strip[:, 3 * P : 4 * P]
 
+        first_copy = keep.tile([P, 2], F32, name="first_copy")
+        nc.vector.memset(first_copy[:], 0.0)
+        nc.scalar.copy(out=first_copy[:, 1:2], in_=first_copy[:, 0:1])
+
         x_rows = keep.tile([P, NODES * 12], BF16, name="x_rows", align_bytes=64)
         x_pairs = keep.tile([P, NODES * 12], BF16, name="x_pairs")
         a_rows = keep.tile([P, TILES * NODES], BF16, name="a_rows")
@@ -99,10 +103,9 @@ def tile_gcn_pa_kernel(tc, a, x, out):
         pair_words = x_pairs[:].bitcast(F32)
         x_banks = {}
 
-        def x_pair_up(g, half):
+        def x_pair_up(g, half, r, engine):
             part = slice(half * P // 2, (half + 1) * P // 2)
-            for r in range(3):
-                nc.vector.tensor_copy(out=x_by_place[:, g, r, :, part], in_=x_by_node[:, g, r, :, part])
+            copy(engine, x_by_place[:, g, r, :, part], x_by_node[:, g, r, :, part])
 
         def x_transposes(g):
             for h in range(STEP_PAIRS):
@@ -128,26 +131,30 @@ def tile_gcn_pa_kernel(tc, a, x, out):
         a_words = a_rows[:].bitcast(F32)
         left_words = left_grouped[:].bitcast(F32)
 
-        def left_tile(tau):
+        left_banks = {}
+
+        def left_transposes(tau):
             bank = new_bank()
+            left_banks[tau] = bank
             for i in range(4):
                 first = tau * ROW_WORDS + i // 2 * 2 * P
                 nc.tensor.transpose(bank[:, i * P : (i + 1) * P], a_words[:, first + i % 2 : first + 2 * P : 2], identity)
+
+        def left_regroup(tau):
             copy(
                 "scalar",
                 left_words[:, tau * ROW_WORDS : (tau + 1) * ROW_WORDS].rearrange("p (g n u) -> p g n u", g=PASSES, u=2),
-                bank[:].rearrange("p (g u n) -> p g n u", g=PASSES, u=2),
+                left_banks[tau][:].rearrange("p (g u n) -> p g n u", g=PASSES, u=2),
             )
 
         def left_quantise(tau):
-            quantise(left_mx[0], left_mx[1], left_grouped, tau * PASSES * P, PASSES * P)
+            quantise(left_mx[0], left_mx[1], left_grouped, tau * PASSES * P, 2 * PASSES * P)
 
-        half_tile = P // 2
-        a_by_tile = a_rows[:].rearrange("p (g t q n e) -> p g q n e t", g=PASSES, t=SLOTS, q=4, n=half_tile, e=SLOTS)
-        right_by_tile = right_grouped[:].rearrange("p (g h e m n t) -> p g h m n e t", g=PASSES, h=PASSES, e=SLOTS, m=2, n=half_tile, t=SLOTS)
+        a_by_tile = a_rows[:].rearrange("p (g t h n e) -> p g h n e t", g=PASSES, t=SLOTS, h=PASSES, n=P, e=SLOTS)
+        right_by_tile = right_grouped[:].rearrange("p (g h e n t) -> p g h n e t", g=PASSES, h=PASSES, e=SLOTS, n=P, t=SLOTS)
 
-        def right_regroup(g, q):
-            nc.vector.tensor_copy(out=right_by_tile[:, g, q // 2, q % 2], in_=a_by_tile[:, g, q])
+        def right_regroup(g, h):
+            nc.vector.tensor_copy(out=right_by_tile[:, g, h], in_=a_by_tile[:, g, h])
 
         result_tiles = {}
 
@@ -166,6 +173,22 @@ def tile_gcn_pa_kernel(tc, a, x, out):
             if c == CHUNKS - 1:
                 rows = out[:, term].rearrange("b (g p t) c l -> g t p b (c l)", g=PASSES, p=P, t=SLOTS)[tau // SLOTS, tau % SLOTS]
                 nc.sync.dma_start(out=rows, in_=result[:].rearrange("p (b f) -> p b f", b=4))
+
+        def y_last_half(tau, half):
+            result = results.tile([P, COLS // 2], F32, name="result", tag="result")
+            for pair, pairs, engine in ((0, 4, "vector"), (4, 2, "scalar")):
+                bank = new_bank()
+                for j in range(pairs):
+                    for g in range(PASSES):
+                        first = g * COLS + (2 * (pair + j) + half) * P
+                        mx_pass(bank[:, j * P : (j + 1) * P], t2_mx, (tau * PASSES + g) * P, x_mx, first, P, g)
+                copy(
+                    engine,
+                    result[:].rearrange("p (b l) -> p b l", l=12)[:, :, 2 * pair : 2 * (pair + pairs)].rearrange("p b (h k) -> p b h k", k=2),
+                    bank[:, : pairs * P].rearrange("p (h b k) -> p b h k", h=pairs, k=2),
+                )
+            rows = out[:, 1].rearrange("b (g p t) c l -> g t p b (c l)", g=PASSES, p=P, t=SLOTS)[tau // SLOTS, tau % SLOTS]
+            nc.sync.dma_start(out=rows[:, 2 * half : 2 * half + 2], in_=result[:].rearrange("p (b f) -> p b f", b=2))
 
         def t2_tile(j):
             for g2 in range(PASSES):
@@ -188,53 +211,61 @@ def tile_gcn_pa_kernel(tc, a, x, out):
                     nc.scalar.activation(out=dst, in_=src, func=ACT.Copy, scale=2.0)
             quantise(t2_mx[0], t2_mx[1], t2_grouped, j * PASSES * P, PASSES * P)
 
-        x_pair_up(0, 0)
-        x_pair_up(0, 1)
+        for half in range(2):
+            for r in range(3):
+                x_pair_up(0, half, r, "scalar" if r == 2 else "vector")
         x_transposes(0)
         for h in range(STEP_PAIRS):
             x_regroup(0, h, "scalar")
-        x_pair_up(1, 0)
-        x_pair_up(1, 1)
-        x_quantise(0, 0)
+        for half, r in ((0, 0), (0, 1), (1, 0), (0, 2), (1, 1), (1, 2)):
+            x_pair_up(1, half, r, "vector")
+        for tau in range(2):
+            left_transposes(tau)
+            left_regroup(tau)
         x_transposes(1)
-        x_regroup(1, 0, "scalar")
-        x_regroup(1, 1, "scalar")
-        for tau in range(4):
-            left_tile(tau)
-        x_quantise(1, 0)
+        for tau in (2, 3):
+            left_transposes(tau)
+        x_quantise(0, 0)
         left_quantise(0)
-        left_quantise(1)
-        x_regroup(1, 2, "scalar")
-        x_regroup(1, 3, "vector")
-        left_quantise(2)
-        left_quantise(3)
-        x_quantise(0, 1)
-        x_quantise(1, 1)
-        x_regroup(1, 4, "scalar")
-        x_regroup(1, 5, "vector")
-        x_quantise(0, 2)
-        x_quantise(1, 2)
-        for tau in range(4):
+        for c in range(CHUNKS):
+            x_regroup(1, 2 * c, "vector" if c == 1 else "scalar")
+            x_regroup(1, 2 * c + 1, "scalar")
+            x_quantise(1, c)
+            if c < CHUNKS - 1:
+                x_quantise(0, c + 1)
+        for tau in range(2):
             y_chunk(0, tau, 0, left_mx, "scalar")
-        for q in range(4):
-            right_regroup(0, q)
+        for tau in (2, 3):
+            left_regroup(tau)
+        left_quantise(2)
         for tau in range(4, TILES):
-            left_tile(tau)
-        for tau in range(4, TILES):
-            left_quantise(tau)
-        for c in range(1, CHUNKS):
-            for tau in range(4):
-                y_chunk(0, tau, c, left_mx, "scalar")
-        for q in range(4):
-            right_regroup(1, q)
-        for g in range(PASSES):
-            quantise(right_mx[0], right_mx[1], right_grouped, g * NODES, NODES)
-        for tau in range(4, TILES):
+            left_transposes(tau)
+        for tau in range(2):
+            y_chunk(0, tau, 1, left_mx, "vector")
+        for tau in (4, 5):
+            left_regroup(tau)
+        for tau in range(2):
+            y_chunk(0, tau, 2, left_mx, "scalar")
+        right_regroup(0, 0)
+        for tau in (6, 7):
+            left_regroup(tau)
+        left_quantise(4)
+        for tau in range(2, TILES):
+            if tau == 3:
+                left_quantise(6)
+            if tau in (2, 4, 5):
+                right_regroup(*{2: (0, 1), 4: (1, 0), 5: (1, 1)}[tau])
+            if tau in (3, 5):
+                g = tau // 2 - 1
+                quantise(right_mx[0], right_mx[1], right_grouped, g * NODES, NODES)
             for c in range(CHUNKS):
-                y_chunk(0, tau, c, left_mx, "scalar" if tau < TILES - 1 else "vector")
-        for j in range(TILES + 1):
-            if j < TILES:
-                t2_tile(j)
-            if j > 0:
+                on_vector = (tau, c) in ((6, 1), (7, 0), (7, 2))
+                y_chunk(0, tau, c, left_mx, "vector" if on_vector else "scalar")
+        for j in range(TILES):
+            t2_tile(j)
+            if 0 < j < TILES - 1:
                 for c in range(CHUNKS):
                     y_chunk(1, j - 1, c, t2_mx, "vector" if (j - 1) % 3 == 1 else "scalar")
+        for tau in (TILES - 2, TILES - 1):
+            for half in range(2):
+                y_last_half(tau, half)

from contextlib import ExitStack

import concourse.mybir as mybir
from concourse.masks import make_identity

F32 = mybir.dt.float32
BF16 = mybir.dt.bfloat16
U32 = mybir.dt.uint32
U8 = mybir.dt.uint8
FP8X4 = mybir.dt.float8_e4m3fn_x4
ALU = mybir.AluOpType
ACT = mybir.ActivationFunctionType

P = 128
TILES = 8
PASSES = 2
SLOTS = 4
NODES = 1024
STEP_PAIRS = 6
COLS = 1536
CHUNK = 512
CHUNKS = COLS // CHUNK
ROW_WORDS = NODES // 2
FLOPS = 2 * NODES * NODES * (NODES + 2 * COLS)


def tile_gcn_pa_kernel(tc, a, x, out):
    nc = tc.nc
    with ExitStack() as ctx:
        ctx.enter_context(tc.manual_schedule())
        keep = ctx.enter_context(tc.tile_pool(name="keep", bufs=1))
        results = ctx.enter_context(tc.tile_pool(name="results", bufs=8))
        psum = ctx.enter_context(tc.psum_pool(name="psum", bufs=8))

        def new_bank():
            bank = psum.tile([P, CHUNK], F32, name="bank", tag="bank")
            return bank

        def copy(engine, dst, src):
            if engine == "vector":
                nc.vector.tensor_copy(out=dst, in_=src)
            else:
                nc.scalar.copy(out=dst, in_=src)

        def quantise(codes, scales, grouped, first, width):
            nc.vector.quantize_mx(
                out=codes[:, first : first + width].bitcast(FP8X4),
                scales=scales[:, first : first + width],
                in_=grouped[:, SLOTS * first : SLOTS * (first + width)],
            )

        def mx_pass(acc, left, left_first, right, right_first, width, g):
            nc.tensor.matmul_mx(
                out=acc,
                lhsT=left[0][:, left_first : left_first + P].bitcast(FP8X4),
                lhsT_scale=left[1][:, left_first : left_first + P],
                rhs=right[0][:, right_first : right_first + width].bitcast(FP8X4),
                rhs_scale=right[1][:, right_first : right_first + width],
                start=(g == 0),
                stop=(g == PASSES - 1),
            )

        eye_strip = keep.tile([P, 7 * P], F32, name="eye_strip")
        nc.gpsimd.memset(eye_strip[:], 0.0)
        make_identity(nc, eye_strip[:, 3 * P : 4 * P], nomemset=True)
        identity = eye_strip[:, 3 * P : 4 * P]

        first_copy = keep.tile([P, 2], F32, name="first_copy")
        nc.vector.memset(first_copy[:], 0.0)
        nc.scalar.copy(out=first_copy[:, 1:2], in_=first_copy[:, 0:1])

        x_rows = keep.tile([P, NODES * 12], BF16, name="x_rows", align_bytes=64)
        x_pairs = keep.tile([P, NODES * 12], BF16, name="x_pairs")
        a_rows = keep.tile([P, TILES * NODES], BF16, name="a_rows")
        x_flat = x.rearrange("b c m l -> (b c) (m l)")
        for q in range(4):
            piece = slice(3072 * q, 3072 * (q + 1))
            nc.sync.dma_start(out=x_rows[:, piece], in_=x_flat[:, piece])
        for q in range(4):
            g, u = q // 2, q % 2
            nc.sync.dma_start(
                out=a_rows[:, 2048 * q : 2048 * (q + 1)].rearrange("p (e m) -> p e m", e=2),
                in_=a[512 * g : 512 * (g + 1), :].rearrange("(p t) m -> p t m", t=SLOTS)[:, 2 * u : 2 * u + 2, :],
            )

        def operand(name, columns):
            grouped = keep.tile([P, SLOTS * columns], BF16, name=name + "_grouped", align_bytes=64)
            codes = keep.tile([P, columns], U32, name=name + "_codes", align_bytes=64)
            scales = keep.tile([P, columns], U8, name=name + "_scales", align_bytes=64)
            return grouped, (codes, scales)

        x_mx = (
            keep.tile([P, PASSES * COLS], U32, name="x_codes", align_bytes=64),
            keep.tile([P, PASSES * COLS], U8, name="x_scales", align_bytes=64),
        )
        x_grouped = x_rows
        left_grouped, left_mx = operand("left", PASSES * NODES)
        right_grouped, right_mx = operand("right", PASSES * NODES)
        t2_grouped, t2_mx = operand("t2", PASSES * NODES)

        x_by_node = x_rows[:].rearrange("b (g p u e r i) -> b g r u p e i", g=PASSES, p=P, u=2, e=2, r=3, i=4)
        x_by_place = x_pairs[:].rearrange("b (g r i u p e) -> b g r u p e i", g=PASSES, r=3, i=4, u=2, p=P, e=2)
        pair_words = x_pairs[:].bitcast(F32)
        x_banks = {}

        def x_pair_up(g, half, r, engine):
            part = slice(half * P // 2, (half + 1) * P // 2)
            copy(engine, x_by_place[:, g, r, :, part], x_by_node[:, g, r, :, part])

        def x_transposes(g):
            for h in range(STEP_PAIRS):
                bank = new_bank()
                x_banks[(g, h)] = bank
                for i in range(4):
                    first = ((g * STEP_PAIRS + h) * 4 + i) * P
                    nc.tensor.transpose(bank[:, i * P : (i + 1) * P], pair_words[:, first : first + P], identity)

        x_words = x_grouped[:].bitcast(F32)

        def x_regroup(g, h, engine):
            first = 2 * (g * COLS + h * 2 * P)
            copy(
                engine,
                x_words[:, first : first + CHUNK].rearrange("p (b k u) -> p b k u", k=2, u=2),
                x_banks[(g, h)][:].rearrange("p (k u b) -> p b k u", k=2, u=2),
            )

        def x_quantise(g, c):
            quantise(x_mx[0], x_mx[1], x_grouped, g * COLS + c * CHUNK, CHUNK)

        a_words = a_rows[:].bitcast(F32)
        left_words = left_grouped[:].bitcast(F32)

        left_banks = {}

        def left_transposes(tau):
            bank = new_bank()
            left_banks[tau] = bank
            for i in range(4):
                first = tau * ROW_WORDS + i // 2 * 2 * P
                nc.tensor.transpose(bank[:, i * P : (i + 1) * P], a_words[:, first + i % 2 : first + 2 * P : 2], identity)

        def left_regroup(tau):
            copy(
                "scalar",
                left_words[:, tau * ROW_WORDS : (tau + 1) * ROW_WORDS].rearrange("p (g n u) -> p g n u", g=PASSES, u=2),
                left_banks[tau][:].rearrange("p (g u n) -> p g n u", g=PASSES, u=2),
            )

        def left_quantise(tau):
            quantise(left_mx[0], left_mx[1], left_grouped, tau * PASSES * P, 2 * PASSES * P)

        a_by_tile = a_rows[:].rearrange("p (g t h n e) -> p g h n e t", g=PASSES, t=SLOTS, h=PASSES, n=P, e=SLOTS)
        right_by_tile = right_grouped[:].rearrange("p (g h e n t) -> p g h n e t", g=PASSES, h=PASSES, e=SLOTS, n=P, t=SLOTS)

        def right_regroup(g, h):
            nc.vector.tensor_copy(out=right_by_tile[:, g, h], in_=a_by_tile[:, g, h])

        result_tiles = {}

        def y_chunk(term, tau, c, left, engine):
            bank = new_bank()
            for g in range(PASSES):
                mx_pass(bank[:], left, (tau * PASSES + g) * P, x_mx, g * COLS + c * CHUNK, CHUNK, g)
            if c == 0:
                result_tiles[(term, tau)] = results.tile([P, COLS], F32, name="result", tag="result")
            result = result_tiles[(term, tau)]
            copy(
                engine,
                result[:].rearrange("p (b l) -> p b l", l=12)[:, :, 4 * c : 4 * c + 4].rearrange("p b (h k) -> p b h k", k=2),
                bank[:].rearrange("p (h b k) -> p b h k", h=2, k=2),
            )
            if c == CHUNKS - 1:
                rows = out[:, term].rearrange("b (g p t) c l -> g t p b (c l)", g=PASSES, p=P, t=SLOTS)[tau // SLOTS, tau % SLOTS]
                nc.sync.dma_start(out=rows, in_=result[:].rearrange("p (b f) -> p b f", b=4))

        def y_last_half(tau, half):
            result = results.tile([P, COLS // 2], F32, name="result", tag="result")
            for pair, pairs, engine in ((0, 4, "vector"), (4, 2, "scalar")):
                bank = new_bank()
                for j in range(pairs):
                    for g in range(PASSES):
                        first = g * COLS + (2 * (pair + j) + half) * P
                        mx_pass(bank[:, j * P : (j + 1) * P], t2_mx, (tau * PASSES + g) * P, x_mx, first, P, g)
                copy(
                    engine,
                    result[:].rearrange("p (b l) -> p b l", l=12)[:, :, 2 * pair : 2 * (pair + pairs)].rearrange("p b (h k) -> p b h k", k=2),
                    bank[:, : pairs * P].rearrange("p (h b k) -> p b h k", h=pairs, k=2),
                )
            rows = out[:, 1].rearrange("b (g p t) c l -> g t p b (c l)", g=PASSES, p=P, t=SLOTS)[tau // SLOTS, tau % SLOTS]
            nc.sync.dma_start(out=rows[:, 2 * half : 2 * half + 2], in_=result[:].rearrange("p (b f) -> p b f", b=2))

        def t2_tile(j):
            for g2 in range(PASSES):
                bank = new_bank()
                for t in range(SLOTS):
                    for g in range(PASSES):
                        mx_pass(bank[:, t * P : (t + 1) * P], right_mx, g * NODES + (SLOTS * g2 + t) * P,
                                left_mx, (j * PASSES + g) * P, P, g)
                first = SLOTS * (j * PASSES + g2) * P
                dst = t2_grouped[:, first : first + SLOTS * P].rearrange("p (n t) -> p n t", t=SLOTS)
                src = bank[:].rearrange("p (t n) -> p n t", t=SLOTS)
                if j // SLOTS == g2:
                    window = (3 - j % SLOTS) * P
                    nc.vector.scalar_tensor_tensor(
                        out=dst, in0=src, scalar=2.0,
                        in1=eye_strip[:, window : window + SLOTS * P].rearrange("p (t n) -> p n t", t=SLOTS),
                        op0=ALU.mult, op1=ALU.subtract,
                    )
                else:
                    nc.scalar.activation(out=dst, in_=src, func=ACT.Copy, scale=2.0)
            quantise(t2_mx[0], t2_mx[1], t2_grouped, j * PASSES * P, PASSES * P)

        for half in range(2):
            for r in range(3):
                x_pair_up(0, half, r, "scalar" if r == 2 else "vector")
        x_transposes(0)
        for h in range(STEP_PAIRS):
            x_regroup(0, h, "scalar")
        for half, r in ((0, 0), (0, 1), (1, 0), (0, 2), (1, 1), (1, 2)):
            x_pair_up(1, half, r, "vector")
        for tau in range(2):
            left_transposes(tau)
            left_regroup(tau)
        x_transposes(1)
        for tau in (2, 3):
            left_transposes(tau)
        x_quantise(0, 0)
        left_quantise(0)
        for c in range(CHUNKS):
            x_regroup(1, 2 * c, "vector" if c == 1 else "scalar")
            x_regroup(1, 2 * c + 1, "scalar")
            x_quantise(1, c)
            if c < CHUNKS - 1:
                x_quantise(0, c + 1)
        for tau in range(2):
            y_chunk(0, tau, 0, left_mx, "scalar")
        for tau in (2, 3):
            left_regroup(tau)
        left_quantise(2)
        for tau in range(4, TILES):
            left_transposes(tau)
        for tau in range(2):
            y_chunk(0, tau, 1, left_mx, "vector")
        for tau in (4, 5):
            left_regroup(tau)
        for tau in range(2):
            y_chunk(0, tau, 2, left_mx, "scalar")
        right_regroup(0, 0)
        for tau in (6, 7):
            left_regroup(tau)
        left_quantise(4)
        for tau in range(2, TILES):
            if tau == 3:
                left_quantise(6)
            if tau in (2, 4, 5):
                right_regroup(*{2: (0, 1), 4: (1, 0), 5: (1, 1)}[tau])
            if tau in (3, 5):
                g = tau // 2 - 1
                quantise(right_mx[0], right_mx[1], right_grouped, g * NODES, NODES)
            for c in range(CHUNKS):
                on_vector = (tau, c) in ((6, 1), (7, 0), (7, 2))
                y_chunk(0, tau, c, left_mx, "vector" if on_vector else "scalar")
        for j in range(TILES):
            t2_tile(j)
            if 0 < j < TILES - 1:
                for c in range(CHUNKS):
                    y_chunk(1, j - 1, c, t2_mx, "vector" if (j - 1) % 3 == 1 else "scalar")
        for tau in (TILES - 2, TILES - 1):
            for half in range(2):
                y_last_half(tau, half)
